import numpy as np
import ml_dtypes


def mxq(x, axis, fmt="e4m3"):
    dtype, down = {"e4m3": (ml_dtypes.float8_e4m3fn, 7), "e5m2": (ml_dtypes.float8_e5m2, 14)}[fmt]
    v = np.moveaxis(np.asarray(x, np.float32).astype(ml_dtypes.bfloat16).astype(np.float64), axis, -1)
    blocks = v.reshape(v.shape[:-1] + (-1, 32))
    amax = np.abs(blocks).max(-1, keepdims=True)
    byte = np.maximum(np.where(amax > 0, np.frexp(amax)[1] - 1 + 127, 0) - down, 1)
    scale = np.exp2(byte - 127.0)
    codes = (blocks / scale).astype(np.float32).astype(dtype).astype(np.float64)
    return np.moveaxis((codes * scale).reshape(v.shape), -1, axis)


WIDE = False


def mx_kscale(k):
    if not WIDE:
        return np.ones(k)
    levels = np.array([10, -10, 5, -5, 0])
    a = np.random.permutation(np.resize(levels, k // 512 * 4)).reshape(k // 512, 4)
    idx = np.arange(k)
    return np.exp2(a[idx // 512, idx % 128 // 32])


BF16 = ml_dtypes.bfloat16


def bf(x):
    return np.asarray(x, np.float32).astype(BF16)


def f64(x):
    return np.asarray(x).astype(np.float64)


N, B, C, E, D, R = 16384, 1024, 512, 128, 128, 8
SPREAD = 2.0


def spread(z, lat):
    return (z[:, :, None] * lat[None, :, :]).sum(1)


def setup_inputs():
    s = mx_kscale(C)
    lat = np.random.standard_normal((R, E)) * SPREAD
    return {
        "source": bf(np.random.standard_normal((N, C)) * s),
        "target": bf(spread(np.random.standard_normal((B, R)), lat)),
        "k_right": bf(spread(np.random.standard_normal((N, R)), lat)),
        "WF_right": bf(np.random.standard_normal((D, C)) * 3.0 / np.sqrt(C) / s),
    }


def reference(source, target, k_right, WF_right):
    t, k = f64(target), f64(k_right)
    f = mxq(f64(source), 1, "e4m3") @ mxq(f64(WF_right).T, 0, "e4m3")
    d2 = (t * t).sum(-1, keepdims=True) + (k * k).sum(-1)[None, :] - 2.0 * (f64(target) @ f64(k_right).T)
    dist = np.sqrt(np.maximum(d2, 0.0))
    l = -dist * E ** (-0.5)
    e = np.exp(l - l.max(-1, keepdims=True))
    return (mxq(e, 1, "e4m3") @ mxq(f, 0, "e4m3")) / e.sum(-1, keepdims=True)

@@ -1,0 +1,413 @@
+from contextlib import ExitStack
+
+import concourse.mybir as mybir
+from concourse.masks import make_identity
+
+F32 = mybir.dt.float32
+BF16 = mybir.dt.bfloat16
+U32 = mybir.dt.uint32
+U8 = mybir.dt.uint8
+FP8X4 = mybir.dt.float8_e4m3fn_x4
+ALU = mybir.AluOpType
+ACT = mybir.ActivationFunctionType
+AX = mybir.AxisListType
+
+P = 128
+N_SRC = 16384
+B_TGT = 1024
+C_IN = 512
+PASS = 512
+N_PASS = N_SRC // PASS
+N_BLK = B_TGT // P
+CHUNK = 2048
+PASS_PER_CHUNK = CHUNK // PASS
+N_CHUNK = N_SRC // CHUNK
+HALF = CHUNK // 2
+N_HALF = N_SRC // HALF
+PAIR = 2
+X_SLOTS = PAIR * N_CHUNK
+E_SLOTS = 6
+DEFER = 5
+SRC_AHEAD = 4
+LOOK = 2
+
+
+FLOPS = 2 * (N_SRC * C_IN * P + 2 * B_TGT * N_SRC * P)
+
+
+def tile_kanadjunction_pa_k_kernel(tc, source, target, k_right, WF_right, out):
+    nc = tc.nc
+    with ExitStack() as ctx:
+        ctx.enter_context(tc.manual_schedule())
+        const = ctx.enter_context(tc.tile_pool(name="const", bufs=1))
+        xpool = ctx.enter_context(tc.tile_pool(name="xpool", bufs=X_SLOTS))
+        work = ctx.enter_context(tc.tile_pool(name="work", bufs=2))
+        small = ctx.enter_context(tc.tile_pool(name="small", bufs=4))
+        psum = ctx.enter_context(tc.psum_pool(name="psum", bufs=8))
+
+        ident_b = const.tile([P, P], BF16, name="ident_b")
+        ident_f = const.tile([P, P], F32, name="ident_f")
+        tTm2 = const.tile([P, B_TGT], BF16, name="tTm2")
+        t2 = const.tile([P, N_BLK], F32, name="t2")
+        negt2 = const.tile([P, N_BLK], F32, name="negt2")
+        t2s = const.tile([P, N_BLK], F32, name="t2s")
+        k2col = const.tile([P, N_SRC // P], F32, name="k2col")
+        kT = const.tile([P, N_SRC], BF16, name="kT")
+        fcodes = const.tile([P, N_PASS * P], U32, name="fcodes", align_bytes=64)
+        fscales = const.tile([P, N_PASS * P], U8, name="fscales", align_bytes=64)
+        wcodes = const.tile([P, P], U32, name="wcodes", align_bytes=64)
+        wscales = const.tile([P, P], U8, name="wscales", align_bytes=64)
+        wgrp = const.tile([P, 4 * P], BF16, name="wgrp", align_bytes=64)
+
+        warm = const.tile([P, 1], F32, name="warm")
+        nc.vector.memset(warm[:], 1.0)
+        nc.scalar.activation(out=warm[:], in_=warm[:], func=ACT.Sqrt)
+        make_identity(nc, ident_b[:])
+        make_identity(nc, ident_f[:])
+
+        kview = k_right.rearrange("(a r u) e -> r a (u e)", a=64, r=P, u=2)
+        kraw = []
+
+        def load_keys(kq):
+            kr = xpool.tile([P, 16, 2 * P], BF16, name="kraw%d" % kq, tag="x")
+            nc.sync.dma_start(out=kr[:], in_=kview[:, 16 * kq : 16 * kq + 16, :])
+            kraw.append(kr)
+
+        kfirst = xpool.tile([P, 16, 2 * P], BF16, name="kraw0", tag="x")
+        kraw.append(kfirst)
+        nc.sync.dma_start(out=kfirst[:, 0:4, :], in_=kview[:, 0:4, :])
+        tg = xpool.tile([P, N_BLK, P], BF16, name="tg", tag="x")
+        nc.sync.dma_start(out=tg[:], in_=target.rearrange("(k p) e -> p k e", p=P))
+        for a0 in (4, 8, 12):
+            nc.sync.dma_start(out=kfirst[:, a0 : a0 + 4, :], in_=kview[:, a0 : a0 + 4, :])
+
+        sview = source.rearrange("(g p i) c -> p g (i c)", g=N_PASS, p=P, i=4)
+        sraw = {}
+
+        def load_source(g):
+            st = work.tile([P, 4 * C_IN], BF16, name="sraw", tag="e", bufs=E_SLOTS, align_bytes=64)
+            nc.sync.dma_start(out=st[:], in_=sview[:, g, :])
+            sraw[g] = st
+
+        wt = xpool.tile([P, C_IN], BF16, name="wt", tag="x")
+        nc.sync.dma_start(out=wt[:], in_=WF_right)
+        for g in range(SRC_AHEAD):
+            load_source(g)
+        load_keys(1)
+
+        def targets():
+            junk = xpool.tile([P, P], F32, name="junk", tag="x")
+            for blk in range(N_BLK):
+                nc.scalar.activation(out=junk[:], in_=tg[:, blk, :], func=ACT.Square, accum_out=t2[:, blk : blk + 1])
+            tp = psum.tile([P, B_TGT], BF16, name="tp", tag="ps")
+            for blk in range(N_BLK):
+                nc.tensor.transpose(tp[:, P * blk : P * blk + P], tg[:, blk, :], ident_b[:])
+            nc.vector.tensor_scalar(out=tTm2[:], in0=tp[:], scalar1=-2.0, scalar2=None, op0=ALU.mult)
+            nc.vector.tensor_scalar(out=negt2[:], in0=t2[:], scalar1=-1.0, scalar2=None, op0=ALU.mult)
+            nc.vector.tensor_scalar(out=t2s[:], in0=t2[:], scalar1=1.0 / P, scalar2=None, op0=ALU.mult)
+
+        ksq = {}
+        ktps = {}
+
+        def key_transpose(hf):
+            ktp = psum.tile([P, HALF], BF16, name="ktp", tag="ps")
+            for gb in range(2):
+                g8 = (2 * hf + gb) % 8
+                for u in range(2):
+                    for h in range(2):
+                        nc.tensor.transpose(
+                            ktp[:, PASS * gb + 256 * u + P * h : PASS * gb + 256 * u + P * h + P],
+                            kraw[hf // 4][:, 2 * g8 + h, P * u : P * u + P],
+                            ident_b[:],
+                        )
+            ktps[hf] = ktp
+
+        def key_square(hf):
+            sq = xpool.tile([P, HALF], F32, name="ksq", tag="x")
+            a0 = 4 * (hf % 4)
+            nc.scalar.activation(
+                out=sq[:].rearrange("p (a w) -> p a w", a=4, w=2 * P), in_=kraw[hf // 4][:, a0 : a0 + 4, :], func=ACT.Square
+            )
+            ksq[hf] = sq
+
+        def key_copy(hf):
+            nc.scalar.copy(out=kT[:, HALF * hf : HALF * hf + HALF], in_=ktps[hf][:])
+
+        def key_norm(hf):
+            nc.vector.tensor_reduce(
+                out=k2col[:, 8 * hf : 8 * hf + 8], in_=ksq[hf][:].rearrange("p (t e) -> p t e", t=8, e=P), axis=AX.X, op=ALU.add
+            )
+
+        def weights():
+            wtp = psum.tile([P, 2, P], F32, name="wtp", tag="ps")
+            ww = wt[:].bitcast(F32)
+            for v in range(2):
+                nc.tensor.transpose(wtp[:, v, :], ww[:, P * v : P * v + P], ident_f[:])
+            nc.vector.tensor_copy(
+                out=wgrp[:].bitcast(F32).rearrange("q (d v) -> q d v", d=P, v=2), in_=wtp[:].rearrange("q v d -> q d v")
+            )
+            nc.vector.quantize_mx(out=wcodes[:].bitcast(FP8X4), scales=wscales[:], in_=wgrp[:])
+
+        sq_tiles = {}
+        fgrp_box = [None]
+
+        def src_transpose(g):
+            sw = sraw[g][:].bitcast(F32)
+            sgrp = work.tile([P, CHUNK], BF16, name="sgrp", tag="grp", align_bytes=64)
+            sgw = sgrp[:].bitcast(F32).rearrange("q (i p v) -> q i p v", i=4, p=P, v=2)
+            for ih in range(2):
+                stp = psum.tile([P, 2, 2, P], F32, name="stp", tag="ps")
+                for a in range(2):
+                    for v in range(2):
+                        w0 = 256 * (2 * ih + a) + P * v
+                        nc.tensor.transpose(stp[:, a, v, :], sw[:, w0 : w0 + P], ident_f[:])
+                nc.scalar.copy(out=sgw[:, 2 * ih : 2 * ih + 2, :, :], in_=stp[:].rearrange("q a v p -> q a p v"))
+            sq_tiles[g] = sgrp
+            if g + SRC_AHEAD < N_PASS:
+                load_source(g + SRC_AHEAD)
+
+        def src_quant(g):
+            scodes = work.tile([P, PASS], U32, name="scodes", tag="codes", bufs=3, align_bytes=64)
+            sscales = work.tile([P, PASS], U8, name="sscales", tag="scales", bufs=3, align_bytes=64)
+            nc.vector.quantize_mx(out=scodes[:].bitcast(FP8X4), scales=sscales[:], in_=sq_tiles[g][:])
+            sq_tiles[g] = (scodes, sscales)
+
+        def src_project(g):
+            scodes, sscales = sq_tiles[g]
+            fps = psum.tile([P, 4, P], F32, name="fps", tag="ps")
+            for i in range(4):
+                t = 2 * (i % 2) + i // 2
+                nc.tensor.matmul_mx(
+                    out=fps[:, t, :],
+                    lhsT=scodes[:, P * i : P * i + P].bitcast(FP8X4),
+                    lhsT_scale=sscales[:, P * i : P * i + P],
+                    rhs=wcodes[:].bitcast(FP8X4),
+                    rhs_scale=wscales[:],
+                    start=True,
+                    stop=True,
+                )
+            full = None
+            if g % PASS_PER_CHUNK == 0:
+                full = fgrp_box[0]
+                fgrp_box[0] = work.tile([P, CHUNK], BF16, name="fgrp", tag="e", bufs=E_SLOTS, align_bytes=64)
+            fg = fgrp_box[0][:].rearrange("p (g d t) -> p g d t", g=PASS_PER_CHUNK, d=P, t=4)
+            nc.vector.tensor_copy(out=fg[:, g % PASS_PER_CHUNK, :, :], in_=fps[:].rearrange("p t d -> p d t"))
+            if g == N_PASS - 1:
+                full = fgrp_box[0]
+            if full is not None:
+                c0 = PASS * ((g - 1) // PASS_PER_CHUNK)
+                nc.vector.quantize_mx(out=fcodes[:, c0 : c0 + PASS].bitcast(FP8X4), scales=fscales[:, c0 : c0 + PASS], in_=full[:])
+
+        def src_unit(g):
+            if g < N_PASS:
+                src_transpose(g)
+            if 1 <= g <= N_PASS:
+                src_quant(g - 1)
+            if 2 <= g <= N_PASS + 1:
+                src_project(g - 2)
+
+        xt = {}
+        mins = {}
+        xmin = {}
+        rs = {}
+        rinv = {}
+        acc = {}
+        sc_tiles = {}
+        e_tiles = {}
+        grp_tiles = {}
+        code_tiles = {}
+
+        def score(i, j):
+            sc = psum.tile([P, PASS], F32, name="sc", tag="ps")
+            nc.tensor.matmul(sc[:], lhsT=tTm2[:, P * i : P * i + P], rhs=kT[:, PASS * j : PASS * j + PASS], start=True, stop=False)
+            sc_tiles[(i, j)] = sc
+
+        def add_norms(i, j):
+            for q in range(4):
+                col = 4 * j + 2 * (q % 2) + q // 2
+                nc.tensor.matmul(
+                    sc_tiles[(i, j)][:, P * q : P * q + P],
+                    lhsT=k2col[:, col : col + 1].to_broadcast([P, P]),
+                    rhs=ident_f[:],
+                    is_transpose=True,
+                    start=False,
+                    stop=(q == 3),
+                )
+
+        def clamp_min(i, j):
+            c, jl = j // PASS_PER_CHUNK, j % PASS_PER_CHUNK
+            if j == 0:
+                mins[i] = small.tile([P, N_PASS], F32, name="mins", tag="mins")
+            if jl == 0:
+                xt[(i, c)] = xpool.tile([P, CHUNK], F32, name="xt", tag="x")
+            nc.vector.tensor_scalar(
+                out=xt[(i, c)][:, PASS * jl : PASS * jl + PASS],
+                in0=sc_tiles[(i, j)][:],
+                scalar1=negt2[:, i : i + 1],
+                scalar2=None,
+                op0=ALU.max,
+                op1=ALU.min,
+                accum_out=mins[i][:, j : j + 1],
+            )
+            if j == N_PASS - 1:
+                mn = small.tile([P, 1], F32, name="mn", tag="mn")
+                nc.vector.tensor_reduce(out=mn[:], in_=mins[i][:], axis=AX.X, op=ALU.min)
+                mins[i] = mn
+
+        def root(i, c):
+            nc.scalar.activation(out=xt[(i, c)][:], in_=xt[(i, c)][:], func=ACT.Sqrt, bias=t2s[:, i : i + 1], scale=1.0 / P)
+            if c == N_CHUNK - 1:
+                xm = small.tile([P, 1], F32, name="xm", tag="xm")
+                nc.scalar.activation(out=xm[:], in_=mins[i][:], func=ACT.Sqrt, bias=t2s[:, i : i + 1], scale=1.0 / P)
+                xmin[i] = xm
+
+        def expo(i, c):
+            if c == 0:
+                rs[i] = small.tile([P, N_CHUNK], F32, name="rs", tag="rs")
+            e = work.tile([P, CHUNK], BF16, name="e", tag="e", bufs=E_SLOTS, align_bytes=64)
+            nc.scalar.activation(
+                out=e[:], in_=xt[(i, c)][:], func=ACT.Exp, bias=xmin[i][:], scale=-1.0, accum_out=rs[i][:, c : c + 1]
+            )
+            e_tiles[(i, c)] = e
+
+        def e_transpose(i, c):
+            ew = e_tiles[(i, c)][:].bitcast(F32)
+            banks = []
+            for hb in range(2):
+                et = psum.tile([P, 2, 2, P], F32, name="et", tag="ps")
+                for a in range(2):
+                    for u in range(2):
+                        w0 = 256 * (2 * hb + a) + P * u
+                        nc.tensor.transpose(et[:, a, u, :], ew[:, w0 : w0 + P], ident_f[:])
+                banks.append(et)
+            e_tiles[(i, c)] = banks
+
+        def e_regroup(i, c):
+            egrp = work.tile([P, CHUNK], BF16, name="egrp", tag="grp", align_bytes=64)
+            egw = egrp[:].bitcast(F32).rearrange("p (g b u) -> p g b u", g=PASS_PER_CHUNK, b=P, u=2)
+            for hb in range(2):
+                nc.vector.tensor_copy(
+                    out=egw[:, 2 * hb : 2 * hb + 2, :, :], in_=e_tiles[(i, c)][hb][:].rearrange("p a u b -> p a b u")
+                )
+            grp_tiles[(i, c)] = egrp
+
+        def e_quant(i, c):
+            ecodes = work.tile([P, PASS], U32, name="ecodes", tag="codes", bufs=3, align_bytes=64)
+            escales = work.tile([P, PASS], U8, name="escales", tag="scales", bufs=3, align_bytes=64)
+            nc.vector.quantize_mx(out=ecodes[:].bitcast(FP8X4), scales=escales[:], in_=grp_tiles[(i, c)][:])
+            code_tiles[(i, c)] = (ecodes, escales)
+
+        def average(i, c):
+            ecodes, escales = code_tiles[(i, c)]
+            if c == 0:
+                acc[i] = psum.tile([P, P], F32, name="acc", tag="ps")
+            for gl in range(PASS_PER_CHUNK):
+                g = PASS_PER_CHUNK * c + gl
+                nc.tensor.matmul_mx(
+                    out=acc[i][:],
+                    lhsT=ecodes[:, P * gl : P * gl + P].bitcast(FP8X4),
+                    lhsT_scale=escales[:, P * gl : P * gl + P],
+                    rhs=fcodes[:, P * g : P * g + P].bitcast(FP8X4),
+                    rhs_scale=fscales[:, P * g : P * g + P],
+                    start=(g == 0),
+                    stop=(g == N_PASS - 1),
+                )
+            if c == N_CHUNK - 1:
+                osb = small.tile([P, P], F32, name="osb", tag="osb", bufs=2)
+                nc.vector.tensor_scalar(out=osb[:], in0=acc[i][:], scalar1=rinv[i][:], scalar2=None, op0=ALU.mult)
+                nc.sync.dma_start(out=out[P * i : P * i + P, :], in_=osb[:])
+
+        def row_sum(i):
+            rtot = small.tile([P, 1], F32, name="rtot", tag="rtot")
+            ri = small.tile([P, 1], F32, name="rinv", tag="rinv")
+            nc.vector.tensor_reduce(out=rtot[:], in_=rs[i][:], axis=AX.X, op=ALU.add)
+            nc.vector.reciprocal(out=ri[:], in_=rtot[:])
+            rinv[i] = ri
+
+
+        for hf in range(2):
+            key_square(hf)
+            key_transpose(hf)
+            key_copy(hf)
+            key_norm(hf)
+            if hf == 0:
+                targets()
+        weights()
+        for hs in range(2 * PAIR * N_CHUNK + 2):
+            t, part = hs // 2, hs % 2
+            i, c = t % PAIR, t // PAIR
+            mine = [(i, PASS_PER_CHUNK * c + 2 * part + jl) for jl in range(2)] if c < N_CHUNK else []
+            for bi, j in mine:
+                score(bi, j)
+            for bi, j in mine:
+                add_norms(bi, j)
+            more_keys = t + 2 < N_HALF
+            if more_keys and part == 0:
+                key_transpose(t + 2)
+            if t >= 1 and part == 0:
+                root((t - 1) % PAIR, (t - 1) // PAIR)
+            if more_keys and part == 0:
+                key_square(t + 2)
+            if more_keys and part == 1:
+                key_copy(t + 2)
+            for bi, j in mine:
+                clamp_min(bi, j)
+            if more_keys and part == 1:
+                key_norm(t + 2)
+            if part == 0 and (t == 1 or t == 5):
+                load_keys(2 + t // 4)
+            src_unit(hs)
+
+        for ph in range(N_BLK // PAIR):
+            chunks = [(PAIR * ph + b, c) for b in range(PAIR) for c in range(N_CHUNK)]
+            last = ph + 1 == N_BLK // PAIR
+            nxt = [] if last else [(PAIR * (ph + 1) + b, j) for b in range(PAIR) for j in range(N_PASS)]
+            n_now = len(chunks) if last else len(chunks) - DEFER
+            scored = [0]
+            done = 0
+
+            def next_scores(limit):
+                n = scored[0]
+                while n < min(len(nxt), limit):
+                    score(nxt[n][0], nxt[n][1])
+                    if n >= 1:
+                        add_norms(nxt[n - 1][0], nxt[n - 1][1])
+                    n += 1
+                if n == len(nxt) and n > scored[0]:
+                    add_norms(nxt[n - 1][0], nxt[n - 1][1])
+                scored[0] = n
+
+            lag = 0 if last else 1
+
+            def regroup_step(k):
+                if k < len(chunks):
+                    e_transpose(chunks[k][0], chunks[k][1])
+                if 0 <= k - lag - 1 < len(chunks):
+                    average(chunks[k - lag - 1][0], chunks[k - lag - 1][1])
+                if k < len(chunks):
+                    if chunks[k][1] == N_CHUNK - 1:
+                        row_sum(chunks[k][0])
+                    e_regroup(chunks[k][0], chunks[k][1])
+                if 0 <= k - lag < len(chunks):
+                    e_quant(chunks[k - lag][0], chunks[k - lag][1])
+
+            for k in range(n_now):
+                expo(chunks[k][0], chunks[k][1])
+                next_scores(min(done + 1 + LOOK, PASS_PER_CHUNK * k))
+                regroup_step(k)
+                if done + 1 < scored[0]:
+                    clamp_min(nxt[done][0], nxt[done][1])
+                    done += 1
+            for k in range(n_now, len(chunks)):
+                expo(chunks[k][0], chunks[k][1])
+            for b in range(done // PASS_PER_CHUNK):
+                root(nxt[PASS_PER_CHUNK * b][0], nxt[PASS_PER_CHUNK * b][1] // PASS_PER_CHUNK)
+            while done < len(nxt):
+                next_scores(done + 2 + LOOK)
+                i, j = nxt[done]
+                clamp_min(i, j)
+                done += 1
+                if j % PASS_PER_CHUNK == PASS_PER_CHUNK - 1:
+                    root(i, j // PASS_PER_CHUNK)
+            for k in range(n_now, len(chunks) + 2):
+                regroup_step(k)

@@ -96,8 +96,8 @@ def tile_kanadjunction_pa_k_kernel(tc, source, target, k_right, WF_right, out):
         load_keys(1)
 
         def targets():
-            junk = xpool.tile([P, P], F32, name="junk", tag="x")
             for blk in range(N_BLK):
+                junk = small.tile([P, P], F32, name="junk", tag="junk")
                 nc.scalar.activation(out=junk[:], in_=tg[:, blk, :], func=ACT.Square, accum_out=t2[:, blk : blk + 1])
             tp = psum.tile([P, B_TGT], BF16, name="tp", tag="ps")
             for blk in range(N_BLK):
@@ -106,7 +106,7 @@ def tile_kanadjunction_pa_k_kernel(tc, source, target, k_right, WF_right, out):
             nc.vector.tensor_scalar(out=negt2[:], in0=t2[:], scalar1=-1.0, scalar2=None, op0=ALU.mult)
             nc.vector.tensor_scalar(out=t2s[:], in0=t2[:], scalar1=1.0 / P, scalar2=None, op0=ALU.mult)
 
-        ksq = {}
+        kst = {}
         ktps = {}
 
         def key_transpose(hf):
@@ -123,19 +123,35 @@ def tile_kanadjunction_pa_k_kernel(tc, source, target, k_right, WF_right, out):
             ktps[hf] = ktp
 
         def key_square(hf):
-            sq = xpool.tile([P, HALF], F32, name="ksq", tag="x")
-            a0 = 4 * (hf % 4)
-            nc.scalar.activation(
-                out=sq[:].rearrange("p (a w) -> p a w", a=4, w=2 * P), in_=kraw[hf // 4][:, a0 : a0 + 4, :], func=ACT.Square
-            )
-            ksq[hf] = sq
+            raw = kraw[hf // 4]
+            for t in range(8):
+                a, u = 4 * (hf % 4) + t // 2, t % 2
+                junk = small.tile([P, P], F32, name="junk", tag="junk")
+                nc.scalar.activation(
+                    out=junk[:], in_=raw[:, a, P * u : P * u + P], func=ACT.Square, accum_out=k2col[:, 8 * hf + t : 8 * hf + t + 1]
+                )
+
+        def key_stats(hf):
+            raw = kraw[hf // 4]
+            st = small.tile([P, 4, 2, 3], F32, name="kst", tag="kst")
+            for a in range(4):
+                nc.vector.bn_stats(
+                    out=st[:, a, :, :].rearrange("p u s -> p (u s)"),
+                    in_=raw[:, 4 * (hf % 4) + a, :].rearrange("p (u e) -> p e u", u=2, e=P),
+                )
+            kst[hf] = st
 
         def key_copy(hf):
             nc.scalar.copy(out=kT[:, HALF * hf : HALF * hf + HALF], in_=ktps[hf][:])
 
         def key_norm(hf):
-            nc.vector.tensor_reduce(
-                out=k2col[:, 8 * hf : 8 * hf + 8], in_=ksq[hf][:].rearrange("p (t e) -> p t e", t=8, e=P), axis=AX.X, op=ALU.add
+            st = kst[hf]
+            sq = small.tile([P, 4, 2], F32, name="ksq", tag="ksq")
+            nc.vector.scalar_tensor_tensor(
+                out=sq[:], in0=st[:, :, :, 1], scalar=float(P), in1=st[:, :, :, 1], op0=ALU.mult, op1=ALU.mult
+            )
+            nc.vector.tensor_tensor(
+                out=k2col[:, 8 * hf : 8 * hf + 8].rearrange("p (a u) -> p a u", a=4, u=2), in0=sq[:], in1=st[:, :, :, 2], op=ALU.add
             )
 
         def weights():
@@ -189,7 +205,7 @@ def tile_kanadjunction_pa_k_kernel(tc, source, target, k_right, WF_right, out):
             full = None
             if g % PASS_PER_CHUNK == 0:
                 full = fgrp_box[0]
-                fgrp_box[0] = work.tile([P, CHUNK], BF16, name="fgrp", tag="e", bufs=E_SLOTS, align_bytes=64)
+                fgrp_box[0] = work.tile([P, CHUNK], BF16, name="fgrp", tag="f", bufs=2, align_bytes=64)
             fg = fgrp_box[0][:].rearrange("p (g d t) -> p g d t", g=PASS_PER_CHUNK, d=P, t=4)
             nc.vector.tensor_copy(out=fg[:, g % PASS_PER_CHUNK, :, :], in_=fps[:].rearrange("p t d -> p d t"))
             if g == N_PASS - 1:
@@ -326,10 +342,14 @@ def tile_kanadjunction_pa_k_kernel(tc, source, target, k_right, WF_right, out):
 
 
         for hf in range(2):
-            key_square(hf)
             key_transpose(hf)
+            if hf % 2 == 1:
+                key_square(hf)
+            else:
+                key_stats(hf)
             key_copy(hf)
-            key_norm(hf)
+            if hf % 2 == 0:
+                key_norm(hf)
             if hf == 0:
                 targets()
         weights()
@@ -346,13 +366,15 @@ def tile_kanadjunction_pa_k_kernel(tc, source, target, k_right, WF_right, out):
                 key_transpose(t + 2)
             if t >= 1 and part == 0:
                 root((t - 1) % PAIR, (t - 1) // PAIR)
-            if more_keys and part == 0:
+            if more_keys and part == 0 and t % 2 == 1:
                 key_square(t + 2)
             if more_keys and part == 1:
                 key_copy(t + 2)
             for bi, j in mine:
                 clamp_min(bi, j)
-            if more_keys and part == 1:
+            if more_keys and part == 0 and t % 2 == 0:
+                key_stats(t + 2)
+            if more_keys and part == 1 and t % 2 == 0:
                 key_norm(t + 2)
             if part == 0 and (t == 1 or t == 5):
                 load_keys(2 + t // 4)

@@ -27,6 +27,8 @@ N_HALF = N_SRC // HALF
 PAIR = 2
 X_SLOTS = PAIR * N_CHUNK
 E_SLOTS = 6
+LAST_BANK = (N_BLK - 1, N_PASS - 2)
+TAIL = (2, 2)
 DEFER = 5
 SRC_AHEAD = 4
 LOOK = 2
@@ -103,6 +105,8 @@ def tile_kanadjunction_pa_k_kernel(tc, source, target, k_right, WF_right, out):
             for blk in range(N_BLK):
                 nc.tensor.transpose(tp[:, P * blk : P * blk + P], tg[:, blk, :], ident_b[:])
             nc.vector.tensor_scalar(out=tTm2[:], in0=tp[:], scalar1=-2.0, scalar2=None, op0=ALU.mult)
+
+        def target_norms():
             nc.vector.tensor_scalar(out=negt2[:], in0=t2[:], scalar1=-1.0, scalar2=None, op0=ALU.mult)
             nc.vector.tensor_scalar(out=t2s[:], in0=t2[:], scalar1=1.0 / P, scalar2=None, op0=ALU.mult)
 
@@ -226,10 +230,12 @@ def tile_kanadjunction_pa_k_kernel(tc, source, target, k_right, WF_right, out):
         mins = {}
         xmin = {}
         rs = {}
+        n_sums = {}
         rinv = {}
         acc = {}
         sc_tiles = {}
         e_tiles = {}
+        e_banks = {}
         grp_tiles = {}
         code_tiles = {}
 
@@ -277,48 +283,61 @@ def tile_kanadjunction_pa_k_kernel(tc, source, target, k_right, WF_right, out):
                 nc.scalar.activation(out=xm[:], in_=mins[i][:], func=ACT.Sqrt, bias=t2s[:, i : i + 1], scale=1.0 / P)
                 xmin[i] = xm
 
-        def expo(i, c):
-            if c == 0:
-                rs[i] = small.tile([P, N_CHUNK], F32, name="rs", tag="rs")
-            e = work.tile([P, CHUNK], BF16, name="e", tag="e", bufs=E_SLOTS, align_bytes=64)
+        def expo(i, g0, n):
+            c, p0 = g0 // PASS_PER_CHUNK, g0 % PASS_PER_CHUNK
+            if g0 == 0:
+                rs[i] = small.tile([P, N_CHUNK + len(TAIL)], F32, name="rs", tag="rs")
+                n_sums[i] = 0
+            if p0 == 0:
+                e_tiles[(i, c)] = work.tile([P, CHUNK], BF16, name="e", tag="e", bufs=E_SLOTS, align_bytes=64)
+            cols = slice(PASS * p0, PASS * (p0 + n))
             nc.scalar.activation(
-                out=e[:], in_=xt[(i, c)][:], func=ACT.Exp, bias=xmin[i][:], scale=-1.0, accum_out=rs[i][:, c : c + 1]
+                out=e_tiles[(i, c)][:, cols],
+                in_=xt[(i, c)][:, cols],
+                func=ACT.Exp,
+                bias=xmin[i][:],
+                scale=-1.0,
+                accum_out=rs[i][:, n_sums[i] : n_sums[i] + 1],
             )
-            e_tiles[(i, c)] = e
+            n_sums[i] += 1
 
-        def e_transpose(i, c):
-            ew = e_tiles[(i, c)][:].bitcast(F32)
+        def e_transpose(i, g0, n):
+            ew = e_tiles[(i, g0 // PASS_PER_CHUNK)][:].bitcast(F32)
             banks = []
-            for hb in range(2):
+            for g in range(g0, g0 + n, 2):
                 et = psum.tile([P, 2, 2, P], F32, name="et", tag="ps")
-                for a in range(2):
+                for a in range(min(2, n)):
                     for u in range(2):
-                        w0 = 256 * (2 * hb + a) + P * u
+                        w0 = 256 * ((g + a) % PASS_PER_CHUNK) + P * u
                         nc.tensor.transpose(et[:, a, u, :], ew[:, w0 : w0 + P], ident_f[:])
                 banks.append(et)
-            e_tiles[(i, c)] = banks
+            e_banks[(i, g0)] = banks
 
-        def e_regroup(i, c):
+        def e_regroup(i, g0, n):
             egrp = work.tile([P, CHUNK], BF16, name="egrp", tag="grp", align_bytes=64)
             egw = egrp[:].bitcast(F32).rearrange("p (g b u) -> p g b u", g=PASS_PER_CHUNK, b=P, u=2)
-            for hb in range(2):
-                nc.vector.tensor_copy(
-                    out=egw[:, 2 * hb : 2 * hb + 2, :, :], in_=e_tiles[(i, c)][hb][:].rearrange("p a u b -> p a b u")
+            w = min(2, n)
+            for hb, et in enumerate(e_banks[(i, g0)]):
+                copy = nc.scalar.copy if (i, g0 + 2 * hb) == LAST_BANK else nc.vector.tensor_copy
+                copy(
+                    out=egw[:, 2 * hb : 2 * hb + w, :, :], in_=et[:, 0:w, :, :].rearrange("p a u b -> p a b u")
                 )
-            grp_tiles[(i, c)] = egrp
+            grp_tiles[(i, g0)] = egrp
 
-        def e_quant(i, c):
+        def e_quant(i, g0, n):
             ecodes = work.tile([P, PASS], U32, name="ecodes", tag="codes", bufs=3, align_bytes=64)
             escales = work.tile([P, PASS], U8, name="escales", tag="scales", bufs=3, align_bytes=64)
-            nc.vector.quantize_mx(out=ecodes[:].bitcast(FP8X4), scales=escales[:], in_=grp_tiles[(i, c)][:])
-            code_tiles[(i, c)] = (ecodes, escales)
+            nc.vector.quantize_mx(
+                out=ecodes[:, 0 : P * n].bitcast(FP8X4), scales=escales[:, 0 : P * n], in_=grp_tiles[(i, g0)][:, 0 : PASS * n]
+            )
+            code_tiles[(i, g0)] = (ecodes, escales)
 
-        def average(i, c):
-            ecodes, escales = code_tiles[(i, c)]
-            if c == 0:
+        def average(i, g0, n):
+            ecodes, escales = code_tiles[(i, g0)]
+            if g0 == 0:
                 acc[i] = psum.tile([P, P], F32, name="acc", tag="ps")
-            for gl in range(PASS_PER_CHUNK):
-                g = PASS_PER_CHUNK * c + gl
+            for gl in range(n):
+                g = g0 + gl
                 nc.tensor.matmul_mx(
                     out=acc[i][:],
                     lhsT=ecodes[:, P * gl : P * gl + P].bitcast(FP8X4),
@@ -328,7 +347,7 @@ def tile_kanadjunction_pa_k_kernel(tc, source, target, k_right, WF_right, out):
                     start=(g == 0),
                     stop=(g == N_PASS - 1),
                 )
-            if c == N_CHUNK - 1:
+            if g0 + n == N_PASS:
                 osb = small.tile([P, P], F32, name="osb", tag="osb", bufs=2)
                 nc.vector.tensor_scalar(out=osb[:], in0=acc[i][:], scalar1=rinv[i][:], scalar2=None, op0=ALU.mult)
                 nc.sync.dma_start(out=out[P * i : P * i + P, :], in_=osb[:])
@@ -336,22 +355,20 @@ def tile_kanadjunction_pa_k_kernel(tc, source, target, k_right, WF_right, out):
         def row_sum(i):
             rtot = small.tile([P, 1], F32, name="rtot", tag="rtot")
             ri = small.tile([P, 1], F32, name="rinv", tag="rinv")
-            nc.vector.tensor_reduce(out=rtot[:], in_=rs[i][:], axis=AX.X, op=ALU.add)
+            nc.vector.tensor_reduce(out=rtot[:], in_=rs[i][:, 0 : n_sums[i]], axis=AX.X, op=ALU.add)
             nc.vector.reciprocal(out=ri[:], in_=rtot[:])
             rinv[i] = ri
 
 
-        for hf in range(2):
-            key_transpose(hf)
-            if hf % 2 == 1:
-                key_square(hf)
-            else:
-                key_stats(hf)
-            key_copy(hf)
-            if hf % 2 == 0:
-                key_norm(hf)
-            if hf == 0:
-                targets()
+        key_transpose(0)
+        key_stats(0)
+        key_copy(0)
+        key_norm(0)
+        targets()
+        target_norms()
+        key_transpose(1)
+        key_square(1)
+        key_copy(1)
         weights()
         for hs in range(2 * PAIR * N_CHUNK + 2):
             t, part = hs // 2, hs % 2
@@ -381,8 +398,13 @@ def tile_kanadjunction_pa_k_kernel(tc, source, target, k_right, WF_right, out):
             src_unit(hs)
 
         for ph in range(N_BLK // PAIR):
-            chunks = [(PAIR * ph + b, c) for b in range(PAIR) for c in range(N_CHUNK)]
+            chunks = [(PAIR * ph + b, PASS_PER_CHUNK * c, PASS_PER_CHUNK) for b in range(PAIR) for c in range(N_CHUNK)]
             last = ph + 1 == N_BLK // PAIR
+            if last:
+                i, g, n = chunks.pop()
+                for n in TAIL:
+                    chunks.append((i, g, n))
+                    g += n
             nxt = [] if last else [(PAIR * (ph + 1) + b, j) for b in range(PAIR) for j in range(N_PASS)]
             n_now = len(chunks) if last else len(chunks) - DEFER
             scored = [0]
@@ -403,25 +425,25 @@ def tile_kanadjunction_pa_k_kernel(tc, source, target, k_right, WF_right, out):
 
             def regroup_step(k):
                 if k < len(chunks):
-                    e_transpose(chunks[k][0], chunks[k][1])
-                if 0 <= k - lag - 1 < len(chunks):
-                    average(chunks[k - lag - 1][0], chunks[k - lag - 1][1])
+                    e_transpose(*chunks[k])
+                if 0 <= k - 2 < len(chunks):
+                    average(*chunks[k - 2])
                 if k < len(chunks):
-                    if chunks[k][1] == N_CHUNK - 1:
-                        row_sum(chunks[k][0])
-                    e_regroup(chunks[k][0], chunks[k][1])
+                    e_regroup(*chunks[k])
                 if 0 <= k - lag < len(chunks):
-                    e_quant(chunks[k - lag][0], chunks[k - lag][1])
+                    e_quant(*chunks[k - lag])
+                if k < len(chunks) and chunks[k][1] + chunks[k][2] == N_PASS:
+                    row_sum(chunks[k][0])
 
             for k in range(n_now):
-                expo(chunks[k][0], chunks[k][1])
+                expo(*chunks[k])
                 next_scores(min(done + 1 + LOOK, PASS_PER_CHUNK * k))
                 regroup_step(k)
                 if done + 1 < scored[0]:
                     clamp_min(nxt[done][0], nxt[done][1])
                     done += 1
             for k in range(n_now, len(chunks)):
-                expo(chunks[k][0], chunks[k][1])
+                expo(*chunks[k])
             for b in range(done // PASS_PER_CHUNK):
                 root(nxt[PASS_PER_CHUNK * b][0], nxt[PASS_PER_CHUNK * b][1] // PASS_PER_CHUNK)
             while done < len(nxt):

@@ -27,10 +27,14 @@ N_HALF = N_SRC // HALF
 PAIR = 2
 X_SLOTS = PAIR * N_CHUNK
 E_SLOTS = 6
-LAST_BANK = (N_BLK - 1, N_PASS - 2)
-TAIL = (2, 2)
 DEFER = 5
 SRC_AHEAD = 4
+FRONT_UNITS = 30
+UNITS_PER_CHUNK = 2
+SC_V = 4
+FQ = 2
+LAST_BANK = (N_BLK - 1, N_PASS - 2)
+TAIL = (2, 2)
 LOOK = 2
 
 
@@ -59,7 +63,6 @@ def tile_kanadjunction_pa_k_kernel(tc, source, target, k_right, WF_right, out):
         fscales = const.tile([P, N_PASS * P], U8, name="fscales", align_bytes=64)
         wcodes = const.tile([P, P], U32, name="wcodes", align_bytes=64)
         wscales = const.tile([P, P], U8, name="wscales", align_bytes=64)
-        wgrp = const.tile([P, 4 * P], BF16, name="wgrp", align_bytes=64)
 
         warm = const.tile([P, 1], F32, name="warm")
         nc.vector.memset(warm[:], 1.0)
@@ -99,14 +102,12 @@ def tile_kanadjunction_pa_k_kernel(tc, source, target, k_right, WF_right, out):
 
         def targets():
             for blk in range(N_BLK):
-                junk = small.tile([P, P], F32, name="junk", tag="junk")
+                junk = small.tile([P, P], BF16, name="junk", tag="junk")
                 nc.scalar.activation(out=junk[:], in_=tg[:, blk, :], func=ACT.Square, accum_out=t2[:, blk : blk + 1])
             tp = psum.tile([P, B_TGT], BF16, name="tp", tag="ps")
             for blk in range(N_BLK):
                 nc.tensor.transpose(tp[:, P * blk : P * blk + P], tg[:, blk, :], ident_b[:])
             nc.vector.tensor_scalar(out=tTm2[:], in0=tp[:], scalar1=-2.0, scalar2=None, op0=ALU.mult)
-
-        def target_norms():
             nc.vector.tensor_scalar(out=negt2[:], in0=t2[:], scalar1=-1.0, scalar2=None, op0=ALU.mult)
             nc.vector.tensor_scalar(out=t2s[:], in0=t2[:], scalar1=1.0 / P, scalar2=None, op0=ALU.mult)
 
@@ -130,7 +131,7 @@ def tile_kanadjunction_pa_k_kernel(tc, source, target, k_right, WF_right, out):
             raw = kraw[hf // 4]
             for t in range(8):
                 a, u = 4 * (hf % 4) + t // 2, t % 2
-                junk = small.tile([P, P], F32, name="junk", tag="junk")
+                junk = small.tile([P, P], BF16, name="junk", tag="junk")
                 nc.scalar.activation(
                     out=junk[:], in_=raw[:, a, P * u : P * u + P], func=ACT.Square, accum_out=k2col[:, 8 * hf + t : 8 * hf + t + 1]
                 )
@@ -159,6 +160,7 @@ def tile_kanadjunction_pa_k_kernel(tc, source, target, k_right, WF_right, out):
             )
 
         def weights():
+            wgrp = work.tile([P, 4 * P], BF16, name="wgrp", tag="sgrp", bufs=2, align_bytes=64)
             wtp = psum.tile([P, 2, P], F32, name="wtp", tag="ps")
             ww = wt[:].bitcast(F32)
             for v in range(2):
@@ -173,7 +175,7 @@ def tile_kanadjunction_pa_k_kernel(tc, source, target, k_right, WF_right, out):
 
         def src_transpose(g):
             sw = sraw[g][:].bitcast(F32)
-            sgrp = work.tile([P, CHUNK], BF16, name="sgrp", tag="grp", align_bytes=64)
+            sgrp = work.tile([P, CHUNK], BF16, name="sgrp", tag="sgrp", bufs=2, align_bytes=64)
             sgw = sgrp[:].bitcast(F32).rearrange("q (i p v) -> q i p v", i=4, p=P, v=2)
             for ih in range(2):
                 stp = psum.tile([P, 2, 2, P], F32, name="stp", tag="ps")
@@ -181,7 +183,10 @@ def tile_kanadjunction_pa_k_kernel(tc, source, target, k_right, WF_right, out):
                     for v in range(2):
                         w0 = 256 * (2 * ih + a) + P * v
                         nc.tensor.transpose(stp[:, a, v, :], sw[:, w0 : w0 + P], ident_f[:])
-                nc.scalar.copy(out=sgw[:, 2 * ih : 2 * ih + 2, :, :], in_=stp[:].rearrange("q a v p -> q a p v"))
+                if 2 * g + ih >= 2 * N_PASS - SC_V:
+                    nc.vector.tensor_copy(out=sgw[:, 2 * ih : 2 * ih + 2, :, :], in_=stp[:].rearrange("q a v p -> q a p v"))
+                else:
+                    nc.scalar.copy(out=sgw[:, 2 * ih : 2 * ih + 2, :, :], in_=stp[:].rearrange("q a v p -> q a p v"))
             sq_tiles[g] = sgrp
             if g + SRC_AHEAD < N_PASS:
                 load_source(g + SRC_AHEAD)
@@ -207,16 +212,18 @@ def tile_kanadjunction_pa_k_kernel(tc, source, target, k_right, WF_right, out):
                     stop=True,
                 )
             full = None
-            if g % PASS_PER_CHUNK == 0:
+            if g % FQ == 0:
                 full = fgrp_box[0]
-                fgrp_box[0] = work.tile([P, CHUNK], BF16, name="fgrp", tag="f", bufs=2, align_bytes=64)
-            fg = fgrp_box[0][:].rearrange("p (g d t) -> p g d t", g=PASS_PER_CHUNK, d=P, t=4)
-            nc.vector.tensor_copy(out=fg[:, g % PASS_PER_CHUNK, :, :], in_=fps[:].rearrange("p t d -> p d t"))
+                fgrp_box[0] = work.tile([P, FQ * PASS], BF16, name="fgrp", tag="f", bufs=2, align_bytes=64)
+            fg = fgrp_box[0][:].rearrange("p (g d t) -> p g d t", g=FQ, d=P, t=4)
+            nc.vector.tensor_copy(out=fg[:, g % FQ, :, :], in_=fps[:].rearrange("p t d -> p d t"))
             if g == N_PASS - 1:
                 full = fgrp_box[0]
             if full is not None:
-                c0 = PASS * ((g - 1) // PASS_PER_CHUNK)
-                nc.vector.quantize_mx(out=fcodes[:, c0 : c0 + PASS].bitcast(FP8X4), scales=fscales[:, c0 : c0 + PASS], in_=full[:])
+                c0 = P * FQ * ((g - 1) // FQ)
+                nc.vector.quantize_mx(
+                    out=fcodes[:, c0 : c0 + P * FQ].bitcast(FP8X4), scales=fscales[:, c0 : c0 + P * FQ], in_=full[:]
+                )
 
         def src_unit(g):
             if g < N_PASS:
@@ -314,7 +321,7 @@ def tile_kanadjunction_pa_k_kernel(tc, source, target, k_right, WF_right, out):
             e_banks[(i, g0)] = banks
 
         def e_regroup(i, g0, n):
-            egrp = work.tile([P, CHUNK], BF16, name="egrp", tag="grp", align_bytes=64)
+            egrp = work.tile([P, CHUNK], BF16, name="egrp", tag="grp", bufs=2, align_bytes=64)
             egw = egrp[:].bitcast(F32).rearrange("p (g b u) -> p g b u", g=PASS_PER_CHUNK, b=P, u=2)
             w = min(2, n)
             for hb, et in enumerate(e_banks[(i, g0)]):
@@ -360,17 +367,26 @@ def tile_kanadjunction_pa_k_kernel(tc, source, target, k_right, WF_right, out):
             rinv[i] = ri
 
 
-        key_transpose(0)
-        key_stats(0)
-        key_copy(0)
-        key_norm(0)
-        targets()
-        target_norms()
-        key_transpose(1)
-        key_square(1)
-        key_copy(1)
+        for hf in range(2):
+            key_transpose(hf)
+            if hf % 2 == 1:
+                key_square(hf)
+            else:
+                key_stats(hf)
+            key_copy(hf)
+            if hf % 2 == 0:
+                key_norm(hf)
+            if hf == 0:
+                targets()
         weights()
-        for hs in range(2 * PAIR * N_CHUNK + 2):
+        units = [0]
+
+        def units_until(n):
+            while units[0] < min(n, N_PASS + 2):
+                src_unit(units[0])
+                units[0] += 1
+
+        for hs in range(2 * PAIR * N_CHUNK + 1):
             t, part = hs // 2, hs % 2
             i, c = t % PAIR, t // PAIR
             mine = [(i, PASS_PER_CHUNK * c + 2 * part + jl) for jl in range(2)] if c < N_CHUNK else []
@@ -395,10 +411,12 @@ def tile_kanadjunction_pa_k_kernel(tc, source, target, k_right, WF_right, out):
                 key_norm(t + 2)
             if part == 0 and (t == 1 or t == 5):
                 load_keys(2 + t // 4)
-            src_unit(hs)
+            units_until((hs + 1) * FRONT_UNITS // (2 * PAIR * N_CHUNK))
 
         for ph in range(N_BLK // PAIR):
             chunks = [(PAIR * ph + b, PASS_PER_CHUNK * c, PASS_PER_CHUNK) for b in range(PAIR) for c in range(N_CHUNK)]
+            if ph == 0:
+                chunks = [(b, PASS_PER_CHUNK * c, PASS_PER_CHUNK) for c in range(N_CHUNK) for b in range(PAIR)]
             last = ph + 1 == N_BLK // PAIR
             if last:
                 i, g, n = chunks.pop()
@@ -437,6 +455,8 @@ def tile_kanadjunction_pa_k_kernel(tc, source, target, k_right, WF_right, out):
 
             for k in range(n_now):
                 expo(*chunks[k])
+                if ph == 0:
+                    units_until(FRONT_UNITS + int((k + 1) * UNITS_PER_CHUNK))
                 next_scores(min(done + 1 + LOOK, PASS_PER_CHUNK * k))
                 regroup_step(k)
                 if done + 1 < scored[0]:

@@ -149,12 +149,16 @@ def tile_kanadjunction_pa_k_kernel(tc, source, target, k_right, WF_right, out):
         def key_copy(hf):
             nc.scalar.copy(out=kT[:, HALF * hf : HALF * hf + HALF], in_=ktps[hf][:])
 
-        def key_norm(hf):
+        def key_means(hf):
             st = kst[hf]
             sq = small.tile([P, 4, 2], F32, name="ksq", tag="ksq")
             nc.vector.scalar_tensor_tensor(
                 out=sq[:], in0=st[:, :, :, 1], scalar=float(P), in1=st[:, :, :, 1], op0=ALU.mult, op1=ALU.mult
             )
+            kst[hf] = (st, sq)
+
+        def key_norm(hf):
+            st, sq = kst[hf]
             nc.vector.tensor_tensor(
                 out=k2col[:, 8 * hf : 8 * hf + 8].rearrange("p (a u) -> p a u", a=4, u=2), in0=sq[:], in1=st[:, :, :, 2], op=ALU.add
             )
@@ -375,6 +379,7 @@ def tile_kanadjunction_pa_k_kernel(tc, source, target, k_right, WF_right, out):
                 key_stats(hf)
             key_copy(hf)
             if hf % 2 == 0:
+                key_means(hf)
                 key_norm(hf)
             if hf == 0:
                 targets()
@@ -397,8 +402,6 @@ def tile_kanadjunction_pa_k_kernel(tc, source, target, k_right, WF_right, out):
             more_keys = t + 2 < N_HALF
             if more_keys and part == 0:
                 key_transpose(t + 2)
-            if t >= 1 and part == 0:
-                root((t - 1) % PAIR, (t - 1) // PAIR)
             if more_keys and part == 0 and t % 2 == 1:
                 key_square(t + 2)
             if more_keys and part == 1:
@@ -411,7 +414,11 @@ def tile_kanadjunction_pa_k_kernel(tc, source, target, k_right, WF_right, out):
                 key_norm(t + 2)
             if part == 0 and (t == 1 or t == 5):
                 load_keys(2 + t // 4)
-            units_until((hs + 1) * FRONT_UNITS // (2 * PAIR * N_CHUNK))
+            units_until(1 + hs * (FRONT_UNITS - 1) // (N_PASS - 1))
+            if t >= 1 and part == 0:
+                root((t - 1) % PAIR, (t - 1) // PAIR)
+            if more_keys and part == 0 and t % 2 == 0:
+                key_means(t + 2)
 
         for ph in range(N_BLK // PAIR):
             chunks = [(PAIR * ph + b, PASS_PER_CHUNK * c, PASS_PER_CHUNK) for b in range(PAIR) for c in range(N_CHUNK)]

@@ -242,6 +242,7 @@ def tile_kanadjunction_pa_k_kernel(tc, source, target, k_right, WF_right, out):
         xmin = {}
         rs = {}
         n_sums = {}
+        rsum = {}
         rinv = {}
         acc = {}
         sc_tiles = {}
@@ -282,17 +283,19 @@ def tile_kanadjunction_pa_k_kernel(tc, source, target, k_right, WF_right, out):
                 op1=ALU.min,
                 accum_out=mins[i][:, j : j + 1],
             )
-            if j == N_PASS - 1:
-                mn = small.tile([P, 1], F32, name="mn", tag="mn")
-                nc.vector.tensor_reduce(out=mn[:], in_=mins[i][:], axis=AX.X, op=ALU.min)
-                mins[i] = mn
+
+        def row_min(i):
+            mn = small.tile([P, 1], F32, name="mn", tag="mn")
+            nc.vector.tensor_reduce(out=mn[:], in_=mins[i][:], axis=AX.X, op=ALU.min)
+            mins[i] = mn
 
         def root(i, c):
             nc.scalar.activation(out=xt[(i, c)][:], in_=xt[(i, c)][:], func=ACT.Sqrt, bias=t2s[:, i : i + 1], scale=1.0 / P)
-            if c == N_CHUNK - 1:
-                xm = small.tile([P, 1], F32, name="xm", tag="xm")
-                nc.scalar.activation(out=xm[:], in_=mins[i][:], func=ACT.Sqrt, bias=t2s[:, i : i + 1], scale=1.0 / P)
-                xmin[i] = xm
+
+        def root_min(i):
+            xm = small.tile([P, 1], F32, name="xm", tag="xm")
+            nc.scalar.activation(out=xm[:], in_=mins[i][:], func=ACT.Sqrt, bias=t2s[:, i : i + 1], scale=1.0 / P)
+            xmin[i] = xm
 
         def expo(i, g0, n):
             c, p0 = g0 // PASS_PER_CHUNK, g0 % PASS_PER_CHUNK
@@ -358,16 +361,20 @@ def tile_kanadjunction_pa_k_kernel(tc, source, target, k_right, WF_right, out):
                     start=(g == 0),
                     stop=(g == N_PASS - 1),
                 )
-            if g0 + n == N_PASS:
-                osb = small.tile([P, P], F32, name="osb", tag="osb", bufs=2)
-                nc.vector.tensor_scalar(out=osb[:], in0=acc[i][:], scalar1=rinv[i][:], scalar2=None, op0=ALU.mult)
-                nc.sync.dma_start(out=out[P * i : P * i + P, :], in_=osb[:])
+
+        def finish(i):
+            osb = small.tile([P, P], F32, name="osb", tag="osb", bufs=2)
+            nc.vector.tensor_scalar(out=osb[:], in0=acc[i][:], scalar1=rinv[i][:], scalar2=None, op0=ALU.mult)
+            nc.sync.dma_start(out=out[P * i : P * i + P, :], in_=osb[:])
 
         def row_sum(i):
             rtot = small.tile([P, 1], F32, name="rtot", tag="rtot")
-            ri = small.tile([P, 1], F32, name="rinv", tag="rinv")
             nc.vector.tensor_reduce(out=rtot[:], in_=rs[i][:, 0 : n_sums[i]], axis=AX.X, op=ALU.add)
-            nc.vector.reciprocal(out=ri[:], in_=rtot[:])
+            rsum[i] = rtot
+
+        def row_inverse(i):
+            ri = small.tile([P, 1], F32, name="rinv", tag="rinv")
+            nc.vector.reciprocal(out=ri[:], in_=rsum[i][:])
             rinv[i] = ri
 
 
@@ -415,8 +422,12 @@ def tile_kanadjunction_pa_k_kernel(tc, source, target, k_right, WF_right, out):
             if part == 0 and (t == 1 or t == 5):
                 load_keys(2 + t // 4)
             units_until(1 + hs * (FRONT_UNITS - 1) // (N_PASS - 1))
+            if mine and mine[-1][1] == N_PASS - 1:
+                row_min(i)
             if t >= 1 and part == 0:
                 root((t - 1) % PAIR, (t - 1) // PAIR)
+                if (t - 1) // PAIR == N_CHUNK - 1:
+                    root_min((t - 1) % PAIR)
             if more_keys and part == 0 and t % 2 == 0:
                 key_means(t + 2)
 
@@ -457,8 +468,9 @@ def tile_kanadjunction_pa_k_kernel(tc, source, target, k_right, WF_right, out):
                     e_regroup(*chunks[k])
                 if 0 <= k - lag < len(chunks):
                     e_quant(*chunks[k - lag])
-                if k < len(chunks) and chunks[k][1] + chunks[k][2] == N_PASS:
-                    row_sum(chunks[k][0])
+                for behind, step in ((0, row_sum), (1, row_inverse), (2, finish)):
+                    if 0 <= k - behind < len(chunks) and chunks[k - behind][1] + chunks[k - behind][2] == N_PASS:
+                        step(chunks[k - behind][0])
 
             for k in range(n_now):
                 expo(*chunks[k])
@@ -480,5 +492,8 @@ def tile_kanadjunction_pa_k_kernel(tc, source, target, k_right, WF_right, out):
                 done += 1
                 if j % PASS_PER_CHUNK == PASS_PER_CHUNK - 1:
                     root(i, j // PASS_PER_CHUNK)
+                if done in (N_PASS + 1, PAIR * N_PASS):
+                    row_min(nxt[done - 2][0])
+                    root_min(nxt[done - 2][0])
             for k in range(n_now, len(chunks) + 2):
                 regroup_step(k)

@@ -29,9 +29,9 @@ X_SLOTS = PAIR * N_CHUNK
 E_SLOTS = 6
 DEFER = 5
 SRC_AHEAD = 4
-FRONT_UNITS = 30
-UNITS_PER_CHUNK = 2
-SC_V = 4
+FRONT_UNITS = 29
+UNITS_PER_CHUNK = 5
+SC_V = 6
 FQ = 2
 LAST_BANK = (N_BLK - 1, N_PASS - 2)
 TAIL = (2, 2)

from contextlib import ExitStack

import concourse.mybir as mybir
from concourse.masks import make_identity

F32 = mybir.dt.float32
BF16 = mybir.dt.bfloat16
U32 = mybir.dt.uint32
U8 = mybir.dt.uint8
FP8X4 = mybir.dt.float8_e4m3fn_x4
ALU = mybir.AluOpType
ACT = mybir.ActivationFunctionType
AX = mybir.AxisListType

P = 128
N_SRC = 16384
B_TGT = 1024
C_IN = 512
PASS = 512
N_PASS = N_SRC // PASS
N_BLK = B_TGT // P
CHUNK = 2048
PASS_PER_CHUNK = CHUNK // PASS
N_CHUNK = N_SRC // CHUNK
HALF = CHUNK // 2
N_HALF = N_SRC // HALF
PAIR = 2
X_SLOTS = PAIR * N_CHUNK
E_SLOTS = 6
DEFER = 5
SRC_AHEAD = 4
FRONT_UNITS = 29
UNITS_PER_CHUNK = 5
SC_V = 6
FQ = 2
LAST_BANK = (N_BLK - 1, N_PASS - 2)
TAIL = (2, 2)
LOOK = 2


FLOPS = 2 * (N_SRC * C_IN * P + 2 * B_TGT * N_SRC * P)


def tile_kanadjunction_pa_k_kernel(tc, source, target, k_right, WF_right, out):
    nc = tc.nc
    with ExitStack() as ctx:
        ctx.enter_context(tc.manual_schedule())
        const = ctx.enter_context(tc.tile_pool(name="const", bufs=1))
        xpool = ctx.enter_context(tc.tile_pool(name="xpool", bufs=X_SLOTS))
        work = ctx.enter_context(tc.tile_pool(name="work", bufs=2))
        small = ctx.enter_context(tc.tile_pool(name="small", bufs=4))
        psum = ctx.enter_context(tc.psum_pool(name="psum", bufs=8))

        ident_b = const.tile([P, P], BF16, name="ident_b")
        ident_f = const.tile([P, P], F32, name="ident_f")
        tTm2 = const.tile([P, B_TGT], BF16, name="tTm2")
        t2 = const.tile([P, N_BLK], F32, name="t2")
        negt2 = const.tile([P, N_BLK], F32, name="negt2")
        t2s = const.tile([P, N_BLK], F32, name="t2s")
        k2col = const.tile([P, N_SRC // P], F32, name="k2col")
        kT = const.tile([P, N_SRC], BF16, name="kT")
        fcodes = const.tile([P, N_PASS * P], U32, name="fcodes", align_bytes=64)
        fscales = const.tile([P, N_PASS * P], U8, name="fscales", align_bytes=64)
        wcodes = const.tile([P, P], U32, name="wcodes", align_bytes=64)
        wscales = const.tile([P, P], U8, name="wscales", align_bytes=64)

        warm = const.tile([P, 1], F32, name="warm")
        nc.vector.memset(warm[:], 1.0)
        nc.scalar.activation(out=warm[:], in_=warm[:], func=ACT.Sqrt)
        make_identity(nc, ident_b[:])
        make_identity(nc, ident_f[:])

        kview = k_right.rearrange("(a r u) e -> r a (u e)", a=64, r=P, u=2)
        kraw = []

        def load_keys(kq):
            kr = xpool.tile([P, 16, 2 * P], BF16, name="kraw%d" % kq, tag="x")
            nc.sync.dma_start(out=kr[:], in_=kview[:, 16 * kq : 16 * kq + 16, :])
            kraw.append(kr)

        kfirst = xpool.tile([P, 16, 2 * P], BF16, name="kraw0", tag="x")
        kraw.append(kfirst)
        nc.sync.dma_start(out=kfirst[:, 0:4, :], in_=kview[:, 0:4, :])
        tg = xpool.tile([P, N_BLK, P], BF16, name="tg", tag="x")
        nc.sync.dma_start(out=tg[:], in_=target.rearrange("(k p) e -> p k e", p=P))
        for a0 in (4, 8, 12):
            nc.sync.dma_start(out=kfirst[:, a0 : a0 + 4, :], in_=kview[:, a0 : a0 + 4, :])

        sview = source.rearrange("(g p i) c -> p g (i c)", g=N_PASS, p=P, i=4)
        sraw = {}

        def load_source(g):
            st = work.tile([P, 4 * C_IN], BF16, name="sraw", tag="e", bufs=E_SLOTS, align_bytes=64)
            nc.sync.dma_start(out=st[:], in_=sview[:, g, :])
            sraw[g] = st

        wt = xpool.tile([P, C_IN], BF16, name="wt", tag="x")
        nc.sync.dma_start(out=wt[:], in_=WF_right)
        for g in range(SRC_AHEAD):
            load_source(g)
        load_keys(1)

        def targets():
            for blk in range(N_BLK):
                junk = small.tile([P, P], BF16, name="junk", tag="junk")
                nc.scalar.activation(out=junk[:], in_=tg[:, blk, :], func=ACT.Square, accum_out=t2[:, blk : blk + 1])
            tp = psum.tile([P, B_TGT], BF16, name="tp", tag="ps")
            for blk in range(N_BLK):
                nc.tensor.transpose(tp[:, P * blk : P * blk + P], tg[:, blk, :], ident_b[:])
            nc.vector.tensor_scalar(out=tTm2[:], in0=tp[:], scalar1=-2.0, scalar2=None, op0=ALU.mult)
            nc.vector.tensor_scalar(out=negt2[:], in0=t2[:], scalar1=-1.0, scalar2=None, op0=ALU.mult)
            nc.vector.tensor_scalar(out=t2s[:], in0=t2[:], scalar1=1.0 / P, scalar2=None, op0=ALU.mult)

        kst = {}
        ktps = {}

        def key_transpose(hf):
            ktp = psum.tile([P, HALF], BF16, name="ktp", tag="ps")
            for gb in range(2):
                g8 = (2 * hf + gb) % 8
                for u in range(2):
                    for h in range(2):
                        nc.tensor.transpose(
                            ktp[:, PASS * gb + 256 * u + P * h : PASS * gb + 256 * u + P * h + P],
                            kraw[hf // 4][:, 2 * g8 + h, P * u : P * u + P],
                            ident_b[:],
                        )
            ktps[hf] = ktp

        def key_square(hf):
            raw = kraw[hf // 4]
            for t in range(8):
                a, u = 4 * (hf % 4) + t // 2, t % 2
                junk = small.tile([P, P], BF16, name="junk", tag="junk")
                nc.scalar.activation(
                    out=junk[:], in_=raw[:, a, P * u : P * u + P], func=ACT.Square, accum_out=k2col[:, 8 * hf + t : 8 * hf + t + 1]
                )

        def key_stats(hf):
            raw = kraw[hf // 4]
            st = small.tile([P, 4, 2, 3], F32, name="kst", tag="kst")
            for a in range(4):
                nc.vector.bn_stats(
                    out=st[:, a, :, :].rearrange("p u s -> p (u s)"),
                    in_=raw[:, 4 * (hf % 4) + a, :].rearrange("p (u e) -> p e u", u=2, e=P),
                )
            kst[hf] = st

        def key_copy(hf):
            nc.scalar.copy(out=kT[:, HALF * hf : HALF * hf + HALF], in_=ktps[hf][:])

        def key_means(hf):
            st = kst[hf]
            sq = small.tile([P, 4, 2], F32, name="ksq", tag="ksq")
            nc.vector.scalar_tensor_tensor(
                out=sq[:], in0=st[:, :, :, 1], scalar=float(P), in1=st[:, :, :, 1], op0=ALU.mult, op1=ALU.mult
            )
            kst[hf] = (st, sq)

        def key_norm(hf):
            st, sq = kst[hf]
            nc.vector.tensor_tensor(
                out=k2col[:, 8 * hf : 8 * hf + 8].rearrange("p (a u) -> p a u", a=4, u=2), in0=sq[:], in1=st[:, :, :, 2], op=ALU.add
            )

        def weights():
            wgrp = work.tile([P, 4 * P], BF16, name="wgrp", tag="sgrp", bufs=2, align_bytes=64)
            wtp = psum.tile([P, 2, P], F32, name="wtp", tag="ps")
            ww = wt[:].bitcast(F32)
            for v in range(2):
                nc.tensor.transpose(wtp[:, v, :], ww[:, P * v : P * v + P], ident_f[:])
            nc.vector.tensor_copy(
                out=wgrp[:].bitcast(F32).rearrange("q (d v) -> q d v", d=P, v=2), in_=wtp[:].rearrange("q v d -> q d v")
            )
            nc.vector.quantize_mx(out=wcodes[:].bitcast(FP8X4), scales=wscales[:], in_=wgrp[:])

        sq_tiles = {}
        fgrp_box = [None]

        def src_transpose(g):
            sw = sraw[g][:].bitcast(F32)
            sgrp = work.tile([P, CHUNK], BF16, name="sgrp", tag="sgrp", bufs=2, align_bytes=64)
            sgw = sgrp[:].bitcast(F32).rearrange("q (i p v) -> q i p v", i=4, p=P, v=2)
            for ih in range(2):
                stp = psum.tile([P, 2, 2, P], F32, name="stp", tag="ps")
                for a in range(2):
                    for v in range(2):
                        w0 = 256 * (2 * ih + a) + P * v
                        nc.tensor.transpose(stp[:, a, v, :], sw[:, w0 : w0 + P], ident_f[:])
                if 2 * g + ih >= 2 * N_PASS - SC_V:
                    nc.vector.tensor_copy(out=sgw[:, 2 * ih : 2 * ih + 2, :, :], in_=stp[:].rearrange("q a v p -> q a p v"))
                else:
                    nc.scalar.copy(out=sgw[:, 2 * ih : 2 * ih + 2, :, :], in_=stp[:].rearrange("q a v p -> q a p v"))
            sq_tiles[g] = sgrp
            if g + SRC_AHEAD < N_PASS:
                load_source(g + SRC_AHEAD)

        def src_quant(g):
            scodes = work.tile([P, PASS], U32, name="scodes", tag="codes", bufs=3, align_bytes=64)
            sscales = work.tile([P, PASS], U8, name="sscales", tag="scales", bufs=3, align_bytes=64)
            nc.vector.quantize_mx(out=scodes[:].bitcast(FP8X4), scales=sscales[:], in_=sq_tiles[g][:])
            sq_tiles[g] = (scodes, sscales)

        def src_project(g):
            scodes, sscales = sq_tiles[g]
            fps = psum.tile([P, 4, P], F32, name="fps", tag="ps")
            for i in range(4):
                t = 2 * (i % 2) + i // 2
                nc.tensor.matmul_mx(
                    out=fps[:, t, :],
                    lhsT=scodes[:, P * i : P * i + P].bitcast(FP8X4),
                    lhsT_scale=sscales[:, P * i : P * i + P],
                    rhs=wcodes[:].bitcast(FP8X4),
                    rhs_scale=wscales[:],
                    start=True,
                    stop=True,
                )
            full = None
            if g % FQ == 0:
                full = fgrp_box[0]
                fgrp_box[0] = work.tile([P, FQ * PASS], BF16, name="fgrp", tag="f", bufs=2, align_bytes=64)
            fg = fgrp_box[0][:].rearrange("p (g d t) -> p g d t", g=FQ, d=P, t=4)
            nc.vector.tensor_copy(out=fg[:, g % FQ, :, :], in_=fps[:].rearrange("p t d -> p d t"))
            if g == N_PASS - 1:
                full = fgrp_box[0]
            if full is not None:
                c0 = P * FQ * ((g - 1) // FQ)
                nc.vector.quantize_mx(
                    out=fcodes[:, c0 : c0 + P * FQ].bitcast(FP8X4), scales=fscales[:, c0 : c0 + P * FQ], in_=full[:]
                )

        def src_unit(g):
            if g < N_PASS:
                src_transpose(g)
            if 1 <= g <= N_PASS:
                src_quant(g - 1)
            if 2 <= g <= N_PASS + 1:
                src_project(g - 2)

        xt = {}
        mins = {}
        xmin = {}
        rs = {}
        n_sums = {}
        rsum = {}
        rinv = {}
        acc = {}
        sc_tiles = {}
        e_tiles = {}
        e_banks = {}
        grp_tiles = {}
        code_tiles = {}

        def score(i, j):
            sc = psum.tile([P, PASS], F32, name="sc", tag="ps")
            nc.tensor.matmul(sc[:], lhsT=tTm2[:, P * i : P * i + P], rhs=kT[:, PASS * j : PASS * j + PASS], start=True, stop=False)
            sc_tiles[(i, j)] = sc

        def add_norms(i, j):
            for q in range(4):
                col = 4 * j + 2 * (q % 2) + q // 2
                nc.tensor.matmul(
                    sc_tiles[(i, j)][:, P * q : P * q + P],
                    lhsT=k2col[:, col : col + 1].to_broadcast([P, P]),
                    rhs=ident_f[:],
                    is_transpose=True,
                    start=False,
                    stop=(q == 3),
                )

        def clamp_min(i, j):
            c, jl = j // PASS_PER_CHUNK, j % PASS_PER_CHUNK
            if j == 0:
                mins[i] = small.tile([P, N_PASS], F32, name="mins", tag="mins")
            if jl == 0:
                xt[(i, c)] = xpool.tile([P, CHUNK], F32, name="xt", tag="x")
            nc.vector.tensor_scalar(
                out=xt[(i, c)][:, PASS * jl : PASS * jl + PASS],
                in0=sc_tiles[(i, j)][:],
                scalar1=negt2[:, i : i + 1],
                scalar2=None,
                op0=ALU.max,
                op1=ALU.min,
                accum_out=mins[i][:, j : j + 1],
            )

        def row_min(i):
            mn = small.tile([P, 1], F32, name="mn", tag="mn")
            nc.vector.tensor_reduce(out=mn[:], in_=mins[i][:], axis=AX.X, op=ALU.min)
            mins[i] = mn

        def root(i, c):
            nc.scalar.activation(out=xt[(i, c)][:], in_=xt[(i, c)][:], func=ACT.Sqrt, bias=t2s[:, i : i + 1], scale=1.0 / P)

        def root_min(i):
            xm = small.tile([P, 1], F32, name="xm", tag="xm")
            nc.scalar.activation(out=xm[:], in_=mins[i][:], func=ACT.Sqrt, bias=t2s[:, i : i + 1], scale=1.0 / P)
            xmin[i] = xm

        def expo(i, g0, n):
            c, p0 = g0 // PASS_PER_CHUNK, g0 % PASS_PER_CHUNK
            if g0 == 0:
                rs[i] = small.tile([P, N_CHUNK + len(TAIL)], F32, name="rs", tag="rs")
                n_sums[i] = 0
            if p0 == 0:
                e_tiles[(i, c)] = work.tile([P, CHUNK], BF16, name="e", tag="e", bufs=E_SLOTS, align_bytes=64)
            cols = slice(PASS * p0, PASS * (p0 + n))
            nc.scalar.activation(
                out=e_tiles[(i, c)][:, cols],
                in_=xt[(i, c)][:, cols],
                func=ACT.Exp,
                bias=xmin[i][:],
                scale=-1.0,
                accum_out=rs[i][:, n_sums[i] : n_sums[i] + 1],
            )
            n_sums[i] += 1

        def e_transpose(i, g0, n):
            ew = e_tiles[(i, g0 // PASS_PER_CHUNK)][:].bitcast(F32)
            banks = []
            for g in range(g0, g0 + n, 2):
                et = psum.tile([P, 2, 2, P], F32, name="et", tag="ps")
                for a in range(min(2, n)):
                    for u in range(2):
                        w0 = 256 * ((g + a) % PASS_PER_CHUNK) + P * u
                        nc.tensor.transpose(et[:, a, u, :], ew[:, w0 : w0 + P], ident_f[:])
                banks.append(et)
            e_banks[(i, g0)] = banks

        def e_regroup(i, g0, n):
            egrp = work.tile([P, CHUNK], BF16, name="egrp", tag="grp", bufs=2, align_bytes=64)
            egw = egrp[:].bitcast(F32).rearrange("p (g b u) -> p g b u", g=PASS_PER_CHUNK, b=P, u=2)
            w = min(2, n)
            for hb, et in enumerate(e_banks[(i, g0)]):
                copy = nc.scalar.copy if (i, g0 + 2 * hb) == LAST_BANK else nc.vector.tensor_copy
                copy(
                    out=egw[:, 2 * hb : 2 * hb + w, :, :], in_=et[:, 0:w, :, :].rearrange("p a u b -> p a b u")
                )
            grp_tiles[(i, g0)] = egrp

        def e_quant(i, g0, n):
            ecodes = work.tile([P, PASS], U32, name="ecodes", tag="codes", bufs=3, align_bytes=64)
            escales = work.tile([P, PASS], U8, name="escales", tag="scales", bufs=3, align_bytes=64)
            nc.vector.quantize_mx(
                out=ecodes[:, 0 : P * n].bitcast(FP8X4), scales=escales[:, 0 : P * n], in_=grp_tiles[(i, g0)][:, 0 : PASS * n]
            )
            code_tiles[(i, g0)] = (ecodes, escales)

        def average(i, g0, n):
            ecodes, escales = code_tiles[(i, g0)]
            if g0 == 0:
                acc[i] = psum.tile([P, P], F32, name="acc", tag="ps")
            for gl in range(n):
                g = g0 + gl
                nc.tensor.matmul_mx(
                    out=acc[i][:],
                    lhsT=ecodes[:, P * gl : P * gl + P].bitcast(FP8X4),
                    lhsT_scale=escales[:, P * gl : P * gl + P],
                    rhs=fcodes[:, P * g : P * g + P].bitcast(FP8X4),
                    rhs_scale=fscales[:, P * g : P * g + P],
                    start=(g == 0),
                    stop=(g == N_PASS - 1),
                )

        def finish(i):
            osb = small.tile([P, P], F32, name="osb", tag="osb", bufs=2)
            nc.vector.tensor_scalar(out=osb[:], in0=acc[i][:], scalar1=rinv[i][:], scalar2=None, op0=ALU.mult)
            nc.sync.dma_start(out=out[P * i : P * i + P, :], in_=osb[:])

        def row_sum(i):
            rtot = small.tile([P, 1], F32, name="rtot", tag="rtot")
            nc.vector.tensor_reduce(out=rtot[:], in_=rs[i][:, 0 : n_sums[i]], axis=AX.X, op=ALU.add)
            rsum[i] = rtot

        def row_inverse(i):
            ri = small.tile([P, 1], F32, name="rinv", tag="rinv")
            nc.vector.reciprocal(out=ri[:], in_=rsum[i][:])
            rinv[i] = ri


        for hf in range(2):
            key_transpose(hf)
            if hf % 2 == 1:
                key_square(hf)
            else:
                key_stats(hf)
            key_copy(hf)
            if hf % 2 == 0:
                key_means(hf)
                key_norm(hf)
            if hf == 0:
                targets()
        weights()
        units = [0]

        def units_until(n):
            while units[0] < min(n, N_PASS + 2):
                src_unit(units[0])
                units[0] += 1

        for hs in range(2 * PAIR * N_CHUNK + 1):
            t, part = hs // 2, hs % 2
            i, c = t % PAIR, t // PAIR
            mine = [(i, PASS_PER_CHUNK * c + 2 * part + jl) for jl in range(2)] if c < N_CHUNK else []
            for bi, j in mine:
                score(bi, j)
            for bi, j in mine:
                add_norms(bi, j)
            more_keys = t + 2 < N_HALF
            if more_keys and part == 0:
                key_transpose(t + 2)
            if more_keys and part == 0 and t % 2 == 1:
                key_square(t + 2)
            if more_keys and part == 1:
                key_copy(t + 2)
            for bi, j in mine:
                clamp_min(bi, j)
            if more_keys and part == 0 and t % 2 == 0:
                key_stats(t + 2)
            if more_keys and part == 1 and t % 2 == 0:
                key_norm(t + 2)
            if part == 0 and (t == 1 or t == 5):
                load_keys(2 + t // 4)
            units_until(1 + hs * (FRONT_UNITS - 1) // (N_PASS - 1))
            if mine and mine[-1][1] == N_PASS - 1:
                row_min(i)
            if t >= 1 and part == 0:
                root((t - 1) % PAIR, (t - 1) // PAIR)
                if (t - 1) // PAIR == N_CHUNK - 1:
                    root_min((t - 1) % PAIR)
            if more_keys and part == 0 and t % 2 == 0:
                key_means(t + 2)

        for ph in range(N_BLK // PAIR):
            chunks = [(PAIR * ph + b, PASS_PER_CHUNK * c, PASS_PER_CHUNK) for b in range(PAIR) for c in range(N_CHUNK)]
            if ph == 0:
                chunks = [(b, PASS_PER_CHUNK * c, PASS_PER_CHUNK) for c in range(N_CHUNK) for b in range(PAIR)]
            last = ph + 1 == N_BLK // PAIR
            if last:
                i, g, n = chunks.pop()
                for n in TAIL:
                    chunks.append((i, g, n))
                    g += n
            nxt = [] if last else [(PAIR * (ph + 1) + b, j) for b in range(PAIR) for j in range(N_PASS)]
            n_now = len(chunks) if last else len(chunks) - DEFER
            scored = [0]
            done = 0

            def next_scores(limit):
                n = scored[0]
                while n < min(len(nxt), limit):
                    score(nxt[n][0], nxt[n][1])
                    if n >= 1:
                        add_norms(nxt[n - 1][0], nxt[n - 1][1])
                    n += 1
                if n == len(nxt) and n > scored[0]:
                    add_norms(nxt[n - 1][0], nxt[n - 1][1])
                scored[0] = n

            lag = 0 if last else 1

            def regroup_step(k):
                if k < len(chunks):
                    e_transpose(*chunks[k])
                if 0 <= k - 2 < len(chunks):
                    average(*chunks[k - 2])
                if k < len(chunks):
                    e_regroup(*chunks[k])
                if 0 <= k - lag < len(chunks):
                    e_quant(*chunks[k - lag])
                for behind, step in ((0, row_sum), (1, row_inverse), (2, finish)):
                    if 0 <= k - behind < len(chunks) and chunks[k - behind][1] + chunks[k - behind][2] == N_PASS:
                        step(chunks[k - behind][0])

            for k in range(n_now):
                expo(*chunks[k])
                if ph == 0:
                    units_until(FRONT_UNITS + int((k + 1) * UNITS_PER_CHUNK))
                next_scores(min(done + 1 + LOOK, PASS_PER_CHUNK * k))
                regroup_step(k)
                if done + 1 < scored[0]:
                    clamp_min(nxt[done][0], nxt[done][1])
                    done += 1
            for k in range(n_now, len(chunks)):
                expo(*chunks[k])
            for b in range(done // PASS_PER_CHUNK):
                root(nxt[PASS_PER_CHUNK * b][0], nxt[PASS_PER_CHUNK * b][1] // PASS_PER_CHUNK)
            while done < len(nxt):
                next_scores(done + 2 + LOOK)
                i, j = nxt[done]
                clamp_min(i, j)
                done += 1
                if j % PASS_PER_CHUNK == PASS_PER_CHUNK - 1:
                    root(i, j // PASS_PER_CHUNK)
                if done in (N_PASS + 1, PAIR * N_PASS):
                    row_min(nxt[done - 2][0])
                    root_min(nxt[done - 2][0])
            for k in range(n_now, len(chunks) + 2):
                regroup_step(k)
